import numpy as np
import ml_dtypes


def mxq(x, axis, fmt="e4m3"):
    dtype, down = {"e4m3": (ml_dtypes.float8_e4m3fn, 7), "e5m2": (ml_dtypes.float8_e5m2, 14)}[fmt]
    v = np.moveaxis(np.asarray(x, np.float32).astype(ml_dtypes.bfloat16).astype(np.float64), axis, -1)
    blocks = v.reshape(v.shape[:-1] + (-1, 32))
    amax = np.abs(blocks).max(-1, keepdims=True)
    byte = np.maximum(np.where(amax > 0, np.frexp(amax)[1] - 1 + 127, 0) - down, 1)
    scale = np.exp2(byte - 127.0)
    codes = (blocks / scale).astype(np.float32).astype(dtype).astype(np.float64)
    return np.moveaxis((codes * scale).reshape(v.shape), -1, axis)


WIDE = False


def mx_kscale(k):
    if not WIDE:
        return np.ones(k)
    levels = np.array([10, -10, 5, -5, 0])
    a = np.random.permutation(np.resize(levels, k // 512 * 4)).reshape(k // 512, 4)
    idx = np.arange(k)
    return np.exp2(a[idx // 512, idx % 128 // 32])


BF16 = ml_dtypes.bfloat16


def bf(x):
    return np.asarray(x, np.float32).astype(BF16)


def f64(x):
    return np.asarray(x).astype(np.float64)


S, HID, NH, Q_LORA, KV_LORA, NOPE, ROPE, VDIM, BLK = 512, 2048, 16, 1536, 512, 128, 64, 128, 128
EPS = 1e-6


def blockscale(rows, cols, k, g):
    return bf((np.random.random((rows, cols)) * 0.8 + 0.2) * g / np.sqrt(k))


def dequant(w, s):
    so = np.repeat(s, BLK, axis=0)[: w.shape[0]]
    se = np.repeat(so, BLK, axis=1)[:, : w.shape[1]]
    return w * se


def rmsnorm(x, w):
    var = np.mean(x * x, axis=-1, keepdims=True)
    return x * (1.0 / np.sqrt(var + EPS)) * w


def setup_inputs():
    s, t = mx_kscale(HID), mx_kscale(KV_LORA)
    return {"hidden_states": bf(np.random.standard_normal((S, HID)) * s),
            "wkv_a_lat": bf(np.random.standard_normal((KV_LORA, HID)) / s[None, :]),
            "skv_a_lat": blockscale(KV_LORA // BLK, HID // BLK, HID, 1.0),
            "wkv_b": bf(np.random.standard_normal((NH * (NOPE + VDIM), KV_LORA)) / t[None, :]),
            "skv_b": blockscale(NH * (NOPE + VDIM) // BLK, KV_LORA // BLK, KV_LORA, 2.0),
            "kv_ln_w": bf((1.0 + 0.1 * np.random.standard_normal(KV_LORA)) * t)}


def reference(hidden_states, wkv_a_lat, skv_a_lat, wkv_b, skv_b, kv_ln_w):
    wa = dequant(f64(wkv_a_lat), f64(skv_a_lat))
    lkv = mxq(f64(hidden_states), 1, "e4m3") @ mxq(wa, 1, "e4m3").T
    kv_nope = rmsnorm(lkv, f64(kv_ln_w))
    wb = dequant(f64(wkv_b), f64(skv_b))
    kvb = (mxq(kv_nope, 1, "e4m3") @ mxq(wb, 1, "e4m3").T).reshape(S, NH, NOPE + VDIM)
    return kvb[..., :NOPE], kvb[..., NOPE:]

@@ -1,0 +1,273 @@
+from contextlib import ExitStack
+
+import concourse.mybir as mybir
+from concourse.masks import make_identity
+
+F32 = mybir.dt.float32
+BF16 = mybir.dt.bfloat16
+U32 = mybir.dt.uint32
+U8 = mybir.dt.uint8
+FP8X4 = mybir.dt.float8_e4m3fn_x4
+ACT = mybir.ActivationFunctionType
+ALU = mybir.AluOpType
+
+P = 128
+TOKENS = 512
+HIDDEN = 2048
+LATENT = 512
+HEADS = 16
+HEAD_DIM = 128
+KINDS = 2
+EPS = 1e-6
+
+K_PASS = 512
+PASSES_A = HIDDEN // K_PASS
+TOKEN_TILES = TOKENS // P
+LATENT_TILES = LATENT // P
+HEADS_PER_CHUNK = 4
+CHUNKS_PER_KIND = HEADS // HEADS_PER_CHUNK
+CHUNK = HEADS_PER_CHUNK * HEAD_DIM
+
+FLOPS = 2 * TOKENS * LATENT * HIDDEN + 2 * TOKENS * HEADS * KINDS * HEAD_DIM * LATENT
+
+
+def tile_deepseekv3attention_pb_kernel(
+    tc, hidden_states, wkv_a_lat, skv_a_lat, wkv_b, skv_b, kv_ln_w, out_0, out_1
+):
+    nc = tc.nc
+    with ExitStack() as stack:
+        const = stack.enter_context(tc.tile_pool(name="const", bufs=1))
+        raw = stack.enter_context(tc.tile_pool(name="raw", bufs=1))
+        keep = stack.enter_context(tc.tile_pool(name="keep", bufs=1))
+        work = stack.enter_context(tc.tile_pool(name="work", bufs=2))
+        stats = stack.enter_context(tc.tile_pool(name="stats", bufs=4))
+        outs = stack.enter_context(tc.tile_pool(name="outs", bufs=4))
+        turn = stack.enter_context(tc.psum_pool(name="turn", bufs=4))
+        acc = stack.enter_context(tc.psum_pool(name="acc", bufs=4))
+
+        eps = const.tile([P, 1], F32, name="eps")
+        nc.vector.memset(eps[:], EPS)
+        warm = const.tile([P, 1], F32, name="warm")
+        nc.scalar.activation(out=warm[:], in_=eps[:], func=ACT.Sqrt)
+        ident = const.tile([P, P], F32, name="ident")
+        make_identity(nc, ident[:])
+
+        sa_all = const.tile([P, 64], BF16, name="sa_all")
+        nc.scalar.dma_start(
+            out=sa_all[:], in_=skv_a_lat.rearrange("a b -> (a b)").partition_broadcast(P)
+        )
+        sb_all = const.tile([P, 128], BF16, name="sb_all")
+        nc.gpsimd.dma_start(
+            out=sb_all[:], in_=skv_b.rearrange("a b -> (a b)").partition_broadcast(P)
+        )
+        gain = const.tile([P, LATENT], BF16, name="gain")
+        nc.gpsimd.dma_start(out=gain[:], in_=kv_ln_w.partition_broadcast(P))
+
+        wa_raw = []
+        for r in range(LATENT_TILES):
+            t = raw.tile([P, HIDDEN], BF16, name="wa_raw%d" % r)
+            nc.sync.dma_start(out=t[:], in_=wkv_a_lat[P * r : P * r + P, :])
+            wa_raw.append(t)
+        x_raw = []
+        for m in range(TOKEN_TILES):
+            t = raw.tile([P, HIDDEN], BF16, name="x_raw%d" % m)
+            nc.sync.dma_start(out=t[:], in_=hidden_states[P * m : P * m + P, :])
+            x_raw.append(t)
+        wb_rows = wkv_b.rearrange("(h k p) c -> p k h c", k=KINDS, p=P)
+        chunks = [(kind, hg) for kind in range(KINDS) for hg in range(CHUNKS_PER_KIND)]
+        wb_raw = []
+        for c, (kind, hg) in enumerate(chunks):
+            t = raw.tile([P, HEADS_PER_CHUNK, LATENT], BF16, name="wb_raw%d" % c)
+            h0 = HEADS_PER_CHUNK * hg
+            nc.sync.dma_start(out=t[:], in_=wb_rows[:, kind, h0 : h0 + HEADS_PER_CHUNK, :])
+            wb_raw.append(t)
+
+        sa_k = const.tile([P, LATENT_TILES, PASSES_A, 4], BF16, name="sa_k")
+        sb_k = const.tile([P, HEADS, KINDS, 4], BF16, name="sb_k")
+        for half in range(2):
+            rows = slice(64 * half, 64 * half + 64)
+            nc.vector.tensor_copy(
+                out=sa_k[rows].rearrange("p r g (u e) -> p (r g u) e", e=2),
+                in_=sa_all[rows]
+                .rearrange("p (x h) -> p x h", h=2)[:, :, half : half + 1]
+                .to_broadcast([64, 32, 2]),
+            )
+            nc.vector.tensor_copy(
+                out=sb_k[rows].rearrange("p h k (u e) -> p (h k u) e", e=2),
+                in_=sb_all[rows]
+                .rearrange("p (x h) -> p x h", h=2)[:, :, half : half + 1]
+                .to_broadcast([64, 64, 2]),
+            )
+
+        wa_grouped = keep.tile([P, PASSES_A, LATENT, 4], BF16, name="wa_grouped", align_bytes=64)
+        wa_codes = keep.tile([P, PASSES_A, LATENT], U32, name="wa_codes", align_bytes=64)
+        wa_scales = keep.tile([P, PASSES_A, LATENT], U8, name="wa_scales", align_bytes=64)
+        x_codes = keep.tile([P, TOKEN_TILES, PASSES_A, P], U32, name="x_codes", align_bytes=64)
+        x_scales = keep.tile([P, TOKEN_TILES, PASSES_A, P], U8, name="x_scales", align_bytes=64)
+        h_codes = keep.tile([P, TOKEN_TILES, P], U32, name="h_codes", align_bytes=64)
+        h_scales = keep.tile([P, TOKEN_TILES, P], U8, name="h_scales", align_bytes=64)
+        wb_codes = keep.tile([P, len(chunks), CHUNK], U32, name="wb_codes", align_bytes=64)
+        wb_scales = keep.tile([P, len(chunks), CHUNK], U8, name="wb_scales", align_bytes=64)
+
+        def turn_four(words, first):
+            bank = turn.tile([P, 2, 2, P], F32, tag="turned")
+            for i in range(2):
+                for u in range(2):
+                    nc.tensor.transpose(
+                        bank[:, u, i, :], words[:, first + i, P * u : P * u + P], ident[:]
+                    )
+            return bank
+
+        def prepare_wa(r):
+            words = wa_raw[r][:].bitcast(F32).rearrange("p (g w) -> p g w", g=PASSES_A)
+            for g0 in range(0, PASSES_A, 2):
+                bank = turn_four(words, g0)
+                nc.vector.tensor_tensor(
+                    out=wa_grouped[:, g0 : g0 + 2, P * r : P * r + P, :].rearrange(
+                        "p g j (u e) -> p g j u e", e=2
+                    ),
+                    in0=bank[:].bitcast(BF16).rearrange("p u g (j e) -> p g j u e", e=2),
+                    in1=sa_k[:, r, g0 : g0 + 2, :]
+                    .rearrange("p g (u e) -> p g u e", e=2)
+                    .unsqueeze(2)
+                    .to_broadcast([P, 2, P, 2, 2]),
+                    op=ALU.mult,
+                )
+
+        def quantise_wa(g):
+            nc.vector.quantize_mx(
+                out=wa_codes[:, g, :].bitcast(FP8X4),
+                scales=wa_scales[:, g, :],
+                in_=wa_grouped[:, g, :, :].rearrange("p o t -> p (o t)"),
+            )
+
+        def prepare_x(m):
+            words = x_raw[m][:].bitcast(F32).rearrange("p (g w) -> p g w", g=PASSES_A)
+            x_grouped = work.tile([P, PASSES_A, P, 4], BF16, tag="x_grouped", align_bytes=64)
+            for g0 in range(0, PASSES_A, 2):
+                bank = turn_four(words, g0)
+                nc.scalar.copy(
+                    out=x_grouped[:].bitcast(F32)[:, g0 : g0 + 2, :, :],
+                    in_=bank[:].rearrange("p u g j -> p g j u"),
+                )
+            nc.vector.quantize_mx(
+                out=x_codes[:, m, :, :].rearrange("p g j -> p (g j)").bitcast(FP8X4),
+                scales=x_scales[:, m, :, :].rearrange("p g j -> p (g j)"),
+                in_=x_grouped[:].rearrange("p g j t -> p (g j t)"),
+            )
+
+        h_rows = {}
+
+        def latent(m):
+            lat = acc.tile([P, LATENT], F32, tag="acc")
+            for g in range(PASSES_A):
+                nc.tensor.matmul_mx(
+                    out=lat[:],
+                    lhsT=x_codes[:, m, g, :].bitcast(FP8X4),
+                    lhsT_scale=x_scales[:, m, g, :],
+                    rhs=wa_codes[:, g, :].bitcast(FP8X4),
+                    rhs_scale=wa_scales[:, g, :],
+                    start=(g == 0),
+                    stop=(g == PASSES_A - 1),
+                )
+            squares = stats.tile([P, LATENT], BF16, tag="squares")
+            sum_sq = stats.tile([P, 1], F32, tag="sum_sq")
+            nc.scalar.activation(out=squares[:], in_=lat[:], func=ACT.Square, accum_out=sum_sq[:])
+            rms = stats.tile([P, 1], F32, tag="rms")
+            nc.scalar.activation(
+                out=rms[:], in_=sum_sq[:], func=ACT.Sqrt, scale=1.0 / LATENT, bias=eps[:]
+            )
+            inv_rms = stats.tile([P, 1], F32, tag="inv_rms")
+            nc.vector.reciprocal(out=inv_rms[:], in_=rms[:])
+            h_sb = stats.tile([P, LATENT], BF16, tag="h_sb")
+            nc.vector.scalar_tensor_tensor(
+                out=h_sb[:],
+                in0=lat[:],
+                scalar=inv_rms[:],
+                in1=gain[:],
+                op0=ALU.mult,
+                op1=ALU.mult,
+            )
+            h_rows[m] = h_sb
+
+        def turn_h(m):
+            words = h_rows[m][:].bitcast(F32)
+            bank = turn.tile([P, 2, P], F32, tag="turned")
+            for u in range(2):
+                nc.tensor.transpose(bank[:, u, :], words[:, P * u : P * u + P], ident[:])
+            h_grouped = work.tile([P, P, 4], BF16, tag="h_grouped", align_bytes=64)
+            nc.scalar.copy(
+                out=h_grouped[:].bitcast(F32), in_=bank[:].rearrange("p u j -> p j u")
+            )
+            nc.vector.quantize_mx(
+                out=h_codes[:, m, :].bitcast(FP8X4),
+                scales=h_scales[:, m, :],
+                in_=h_grouped[:].rearrange("p j t -> p (j t)"),
+            )
+
+        def prepare_wb(c):
+            kind, hg = chunks[c]
+            words = wb_raw[c][:].bitcast(F32)
+            wb_grouped = work.tile([P, CHUNK, 4], BF16, tag="wb_grouped", align_bytes=64)
+            for i0 in range(0, HEADS_PER_CHUNK, 2):
+                bank = turn_four(words, i0)
+                h0 = HEADS_PER_CHUNK * hg + i0
+                nc.vector.tensor_tensor(
+                    out=wb_grouped[:, P * i0 : P * i0 + 2 * P, :].rearrange(
+                        "p (i j) (u e) -> p i j u e", i=2, e=2
+                    ),
+                    in0=bank[:].bitcast(BF16).rearrange("p u i (j e) -> p i j u e", e=2),
+                    in1=sb_k[:, h0 : h0 + 2, kind, :]
+                    .rearrange("p i (u e) -> p i u e", e=2)
+                    .unsqueeze(2)
+                    .to_broadcast([P, 2, P, 2, 2]),
+                    op=ALU.mult,
+                )
+            nc.vector.quantize_mx(
+                out=wb_codes[:, c, :].bitcast(FP8X4),
+                scales=wb_scales[:, c, :],
+                in_=wb_grouped[:].rearrange("p o t -> p (o t)"),
+            )
+
+        out_rows = [
+            o.rearrange("(m p) h d -> p m (h d)", p=P) for o in (out_0, out_1)
+        ]
+
+        def project(c):
+            kind, hg = chunks[c]
+            out_sb = outs.tile([P, TOKEN_TILES, CHUNK], F32, tag="out_sb")
+            for m in range(TOKEN_TILES):
+                kv = acc.tile([P, CHUNK], F32, tag="acc")
+                nc.tensor.matmul_mx(
+                    out=kv[:],
+                    lhsT=h_codes[:, m, :].bitcast(FP8X4),
+                    lhsT_scale=h_scales[:, m, :],
+                    rhs=wb_codes[:, c, :].bitcast(FP8X4),
+                    rhs_scale=wb_scales[:, c, :],
+                    start=True,
+                    stop=True,
+                )
+                if m == TOKEN_TILES - 1:
+                    nc.vector.tensor_copy(out=out_sb[:, m, :], in_=kv[:])
+                else:
+                    nc.scalar.copy(out=out_sb[:, m, :], in_=kv[:])
+            nc.sync.dma_start(
+                out=out_rows[kind][:, :, CHUNK * hg : CHUNK * hg + CHUNK], in_=out_sb[:]
+            )
+
+        for r in range(LATENT_TILES):
+            prepare_wa(r)
+        for g in range(PASSES_A):
+            quantise_wa(g)
+        for step in range(TOKEN_TILES + 2):
+            if step < TOKEN_TILES:
+                prepare_x(step)
+            if 1 <= step <= TOKEN_TILES:
+                latent(step - 1)
+            if step >= 2:
+                turn_h(step - 2)
+        for c in range(len(chunks) + 1):
+            if c < len(chunks):
+                prepare_wb(c)
+            if c >= 1:
+                project(c - 1)

@@ -26,6 +26,7 @@ TOKEN_TILES = TOKENS // P
 LATENT_TILES = LATENT // P
 HEADS_PER_CHUNK = 4
 CHUNKS_PER_KIND = HEADS // HEADS_PER_CHUNK
+CHUNKS = KINDS * CHUNKS_PER_KIND
 CHUNK = HEADS_PER_CHUNK * HEAD_DIM
 
 FLOPS = 2 * TOKENS * LATENT * HIDDEN + 2 * TOKENS * HEADS * KINDS * HEAD_DIM * LATENT
@@ -39,29 +40,28 @@ def tile_deepseekv3attention_pb_kernel(
         const = stack.enter_context(tc.tile_pool(name="const", bufs=1))
         raw = stack.enter_context(tc.tile_pool(name="raw", bufs=1))
         keep = stack.enter_context(tc.tile_pool(name="keep", bufs=1))
-        work = stack.enter_context(tc.tile_pool(name="work", bufs=2))
+        work = stack.enter_context(tc.tile_pool(name="work", bufs=3))
         stats = stack.enter_context(tc.tile_pool(name="stats", bufs=4))
-        outs = stack.enter_context(tc.tile_pool(name="outs", bufs=4))
+        outs = stack.enter_context(tc.tile_pool(name="outs", bufs=12))
         turn = stack.enter_context(tc.psum_pool(name="turn", bufs=4))
         acc = stack.enter_context(tc.psum_pool(name="acc", bufs=4))
+        stack.enter_context(tc.manual_schedule())
 
+        small_a = const.tile([P, 64], BF16, name="small_a")
+        nc.vector.memset(small_a[:], 0.0)
+        nc.sync.dma_start(out=small_a[0:1, :], in_=skv_a_lat.rearrange("(o a) b -> o (a b)", o=1))
+        small_b = const.tile([P, 768], BF16, name="small_b")
+        nc.vector.memset(small_b[:], 0.0)
+        nc.scalar.dma_start(out=small_b[0:1, 0:128], in_=skv_b.rearrange("(o a) b -> o (a b)", o=1))
+        nc.scalar.dma_start(out=small_b[0:1, 256:768], in_=kv_ln_w.rearrange("(o c) -> o c", o=1))
+        ones = const.tile([P, P], BF16, name="ones")
+        nc.vector.memset(ones[:], 1.0)
         eps = const.tile([P, 1], F32, name="eps")
         nc.vector.memset(eps[:], EPS)
         warm = const.tile([P, 1], F32, name="warm")
         nc.scalar.activation(out=warm[:], in_=eps[:], func=ACT.Sqrt)
         ident = const.tile([P, P], F32, name="ident")
         make_identity(nc, ident[:])
-
-        sa_all = const.tile([P, 64], BF16, name="sa_all")
-        nc.scalar.dma_start(
-            out=sa_all[:], in_=skv_a_lat.rearrange("a b -> (a b)").partition_broadcast(P)
-        )
-        sb_all = const.tile([P, 128], BF16, name="sb_all")
-        nc.gpsimd.dma_start(
-            out=sb_all[:], in_=skv_b.rearrange("a b -> (a b)").partition_broadcast(P)
-        )
-        gain = const.tile([P, LATENT], BF16, name="gain")
-        nc.gpsimd.dma_start(out=gain[:], in_=kv_ln_w.partition_broadcast(P))
 
         wa_raw = []
         for r in range(LATENT_TILES):
@@ -82,22 +82,31 @@ def tile_deepseekv3attention_pb_kernel(
             nc.sync.dma_start(out=t[:], in_=wb_rows[:, kind, h0 : h0 + HEADS_PER_CHUNK, :])
             wb_raw.append(t)
 
+        def pick_factors(picked, spread, count):
+            for half in range(2):
+                rows = slice(64 * half, 64 * half + 64)
+                nc.vector.tensor_copy(
+                    out=picked[rows],
+                    in_=spread[rows]
+                    .rearrange("p (x h) -> p x h", h=2)[:, :, half : half + 1]
+                    .to_broadcast([64, count, 2]),
+                )
+
         sa_k = const.tile([P, LATENT_TILES, PASSES_A, 4], BF16, name="sa_k")
+        sa_ps = acc.tile([P, 64], F32, tag="acc")
+        nc.tensor.matmul(out=sa_ps[:], lhsT=ones[:], rhs=small_a[:], start=True, stop=True)
+        pick_factors(sa_k[:].rearrange("p r g (u e) -> p (r g u) e", e=2), sa_ps[:], 32)
+
         sb_k = const.tile([P, HEADS, KINDS, 4], BF16, name="sb_k")
-        for half in range(2):
-            rows = slice(64 * half, 64 * half + 64)
-            nc.vector.tensor_copy(
-                out=sa_k[rows].rearrange("p r g (u e) -> p (r g u) e", e=2),
-                in_=sa_all[rows]
-                .rearrange("p (x h) -> p x h", h=2)[:, :, half : half + 1]
-                .to_broadcast([64, 32, 2]),
-            )
-            nc.vector.tensor_copy(
-                out=sb_k[rows].rearrange("p h k (u e) -> p (h k u) e", e=2),
-                in_=sb_all[rows]
-                .rearrange("p (x h) -> p x h", h=2)[:, :, half : half + 1]
-                .to_broadcast([64, 64, 2]),
-            )
+        gain = const.tile([P, LATENT], F32, name="gain")
+
+        def spread_small_b():
+            sb_ps = acc.tile([P, 256], F32, tag="acc")
+            nc.tensor.matmul(out=sb_ps[:], lhsT=ones[:], rhs=small_b[:, 0:256], start=True, stop=True)
+            pick_factors(sb_k[:].rearrange("p h k (u e) -> p (h k u) e", e=2), sb_ps[:, 0:128], 64)
+            gain_ps = acc.tile([P, LATENT], F32, tag="acc")
+            nc.tensor.matmul(out=gain_ps[:], lhsT=ones[:], rhs=small_b[:, 256:768], start=True, stop=True)
+            nc.scalar.copy(out=gain[:], in_=gain_ps[:])
 
         wa_grouped = keep.tile([P, PASSES_A, LATENT, 4], BF16, name="wa_grouped", align_bytes=64)
         wa_codes = keep.tile([P, PASSES_A, LATENT], U32, name="wa_codes", align_bytes=64)
@@ -106,8 +115,8 @@ def tile_deepseekv3attention_pb_kernel(
         x_scales = keep.tile([P, TOKEN_TILES, PASSES_A, P], U8, name="x_scales", align_bytes=64)
         h_codes = keep.tile([P, TOKEN_TILES, P], U32, name="h_codes", align_bytes=64)
         h_scales = keep.tile([P, TOKEN_TILES, P], U8, name="h_scales", align_bytes=64)
-        wb_codes = keep.tile([P, len(chunks), CHUNK], U32, name="wb_codes", align_bytes=64)
-        wb_scales = keep.tile([P, len(chunks), CHUNK], U8, name="wb_scales", align_bytes=64)
+        wb_codes = keep.tile([P, CHUNKS, CHUNK], U32, name="wb_codes", align_bytes=64)
+        wb_scales = keep.tile([P, CHUNKS, CHUNK], U8, name="wb_scales", align_bytes=64)
 
         def turn_four(words, first):
             bank = turn.tile([P, 2, 2, P], F32, tag="turned")
@@ -118,20 +127,22 @@ def tile_deepseekv3attention_pb_kernel(
                     )
             return bank
 
+        def scale_out(bank, factors, grouped):
+            nc.vector.tensor_tensor(
+                out=grouped.rearrange("p i j (u e) -> p i j u e", e=2),
+                in0=bank[:].bitcast(BF16).rearrange("p u i (j e) -> p i j u e", e=2),
+                in1=factors.rearrange("p i (u e) -> p i u e", e=2)
+                .unsqueeze(2)
+                .to_broadcast([P, 2, P, 2, 2]),
+                op=ALU.mult,
+            )
+
         def prepare_wa(r):
             words = wa_raw[r][:].bitcast(F32).rearrange("p (g w) -> p g w", g=PASSES_A)
             for g0 in range(0, PASSES_A, 2):
                 bank = turn_four(words, g0)
-                nc.vector.tensor_tensor(
-                    out=wa_grouped[:, g0 : g0 + 2, P * r : P * r + P, :].rearrange(
-                        "p g j (u e) -> p g j u e", e=2
-                    ),
-                    in0=bank[:].bitcast(BF16).rearrange("p u g (j e) -> p g j u e", e=2),
-                    in1=sa_k[:, r, g0 : g0 + 2, :]
-                    .rearrange("p g (u e) -> p g u e", e=2)
-                    .unsqueeze(2)
-                    .to_broadcast([P, 2, P, 2, 2]),
-                    op=ALU.mult,
+                scale_out(
+                    bank, sa_k[:, r, g0 : g0 + 2, :], wa_grouped[:, g0 : g0 + 2, P * r : P * r + P, :]
                 )
 
         def quantise_wa(g):
@@ -141,19 +152,24 @@ def tile_deepseekv3attention_pb_kernel(
                 in_=wa_grouped[:, g, :, :].rearrange("p o t -> p (o t)"),
             )
 
-        def prepare_x(m):
+        x_grouped = {}
+
+        def turn_x(m):
             words = x_raw[m][:].bitcast(F32).rearrange("p (g w) -> p g w", g=PASSES_A)
-            x_grouped = work.tile([P, PASSES_A, P, 4], BF16, tag="x_grouped", align_bytes=64)
+            grouped = stats.tile([P, PASSES_A, P, 4], BF16, tag="x_grouped", align_bytes=64)
             for g0 in range(0, PASSES_A, 2):
                 bank = turn_four(words, g0)
                 nc.scalar.copy(
-                    out=x_grouped[:].bitcast(F32)[:, g0 : g0 + 2, :, :],
+                    out=grouped[:].bitcast(F32)[:, g0 : g0 + 2, :, :],
                     in_=bank[:].rearrange("p u g j -> p g j u"),
                 )
+            x_grouped[m] = grouped
+
+        def quantise_x(m):
             nc.vector.quantize_mx(
                 out=x_codes[:, m, :, :].rearrange("p g j -> p (g j)").bitcast(FP8X4),
                 scales=x_scales[:, m, :, :].rearrange("p g j -> p (g j)"),
-                in_=x_grouped[:].rearrange("p g j t -> p (g j t)"),
+                in_=x_grouped[m][:].rearrange("p g j t -> p (g j t)"),
             )
 
         h_rows = {}
@@ -190,52 +206,49 @@ def tile_deepseekv3attention_pb_kernel(
             )
             h_rows[m] = h_sb
 
+        h_grouped = {}
+
         def turn_h(m):
             words = h_rows[m][:].bitcast(F32)
-            bank = turn.tile([P, 2, P], F32, tag="turned")
+            bank = acc.tile([P, 2, P], F32, tag="acc")
             for u in range(2):
                 nc.tensor.transpose(bank[:, u, :], words[:, P * u : P * u + P], ident[:])
-            h_grouped = work.tile([P, P, 4], BF16, tag="h_grouped", align_bytes=64)
-            nc.scalar.copy(
-                out=h_grouped[:].bitcast(F32), in_=bank[:].rearrange("p u j -> p j u")
-            )
+            grouped = stats.tile([P, P, 4], BF16, tag="h_grouped", align_bytes=64)
+            nc.scalar.copy(out=grouped[:].bitcast(F32), in_=bank[:].rearrange("p u j -> p j u"))
+            h_grouped[m] = grouped
+
+        def quantise_h(m):
             nc.vector.quantize_mx(
                 out=h_codes[:, m, :].bitcast(FP8X4),
                 scales=h_scales[:, m, :],
-                in_=h_grouped[:].rearrange("p j t -> p (j t)"),
+                in_=h_grouped[m][:].rearrange("p j t -> p (j t)"),
             )
 
-        def prepare_wb(c):
-            kind, hg = chunks[c]
+        wb_banks = {}
+        wb_grouped = {}
+
+        def turn_wb(c):
             words = wb_raw[c][:].bitcast(F32)
-            wb_grouped = work.tile([P, CHUNK, 4], BF16, tag="wb_grouped", align_bytes=64)
-            for i0 in range(0, HEADS_PER_CHUNK, 2):
-                bank = turn_four(words, i0)
-                h0 = HEADS_PER_CHUNK * hg + i0
-                nc.vector.tensor_tensor(
-                    out=wb_grouped[:, P * i0 : P * i0 + 2 * P, :].rearrange(
-                        "p (i j) (u e) -> p i j u e", i=2, e=2
-                    ),
-                    in0=bank[:].bitcast(BF16).rearrange("p u i (j e) -> p i j u e", e=2),
-                    in1=sb_k[:, h0 : h0 + 2, kind, :]
-                    .rearrange("p i (u e) -> p i u e", e=2)
-                    .unsqueeze(2)
-                    .to_broadcast([P, 2, P, 2, 2]),
-                    op=ALU.mult,
-                )
+            wb_banks[c] = [turn_four(words, i0) for i0 in range(0, HEADS_PER_CHUNK, 2)]
+
+        def scale_wb(c):
+            kind, hg = chunks[c]
+            grouped = work.tile([P, HEADS_PER_CHUNK, P, 4], BF16, tag="wb_grouped", align_bytes=64)
+            for b, bank in enumerate(wb_banks[c]):
+                h0 = HEADS_PER_CHUNK * hg + 2 * b
+                scale_out(bank, sb_k[:, h0 : h0 + 2, kind, :], grouped[:, 2 * b : 2 * b + 2, :, :])
+            wb_grouped[c] = grouped
+
+        def quantise_wb(c):
             nc.vector.quantize_mx(
                 out=wb_codes[:, c, :].bitcast(FP8X4),
                 scales=wb_scales[:, c, :],
-                in_=wb_grouped[:].rearrange("p o t -> p (o t)"),
+                in_=wb_grouped[c][:].rearrange("p i j t -> p (i j t)"),
             )
 
-        out_rows = [
-            o.rearrange("(m p) h d -> p m (h d)", p=P) for o in (out_0, out_1)
-        ]
+        kv_banks = {}
 
         def project(c):
-            kind, hg = chunks[c]
-            out_sb = outs.tile([P, TOKEN_TILES, CHUNK], F32, tag="out_sb")
             for m in range(TOKEN_TILES):
                 kv = acc.tile([P, CHUNK], F32, tag="acc")
                 nc.tensor.matmul_mx(
@@ -247,27 +260,53 @@ def tile_deepseekv3attention_pb_kernel(
                     start=True,
                     stop=True,
                 )
-                if m == TOKEN_TILES - 1:
-                    nc.vector.tensor_copy(out=out_sb[:, m, :], in_=kv[:])
-                else:
-                    nc.scalar.copy(out=out_sb[:, m, :], in_=kv[:])
-            nc.sync.dma_start(
-                out=out_rows[kind][:, :, CHUNK * hg : CHUNK * hg + CHUNK], in_=out_sb[:]
-            )
+                kv_banks[m] = kv
+
+        def store(c):
+            kind, hg = chunks[c]
+            h0 = HEADS_PER_CHUNK * hg
+            for m in range(TOKEN_TILES):
+                out_sb = outs.tile([P, CHUNK], F32, tag="out_sb")
+                nc.scalar.copy(out=out_sb[:], in_=kv_banks[m][:])
+                nc.sync.dma_start(
+                    out=(out_0, out_1)[kind][
+                        P * m : P * m + P, h0 : h0 + HEADS_PER_CHUNK, :
+                    ].rearrange("p h d -> p (h d)"),
+                    in_=out_sb[:],
+                )
 
         for r in range(LATENT_TILES):
             prepare_wa(r)
+        spread_small_b()
+        turn_x(0)
+        turn_x(1)
         for g in range(PASSES_A):
             quantise_wa(g)
-        for step in range(TOKEN_TILES + 2):
-            if step < TOKEN_TILES:
-                prepare_x(step)
-            if 1 <= step <= TOKEN_TILES:
-                latent(step - 1)
-            if step >= 2:
-                turn_h(step - 2)
-        for c in range(len(chunks) + 1):
-            if c < len(chunks):
-                prepare_wb(c)
-            if c >= 1:
-                project(c - 1)
+        quantise_x(0)
+        turn_x(2)
+        quantise_x(1)
+        turn_x(3)
+        quantise_x(2)
+        quantise_x(3)
+        for m in range(TOKEN_TILES):
+            latent(m)
+        turn_wb(0)
+        turn_wb(1)
+        for m in range(TOKEN_TILES):
+            turn_h(m)
+        scale_wb(0)
+        quantise_h(0)
+        quantise_h(1)
+        quantise_wb(0)
+        quantise_h(2)
+        quantise_h(3)
+        scale_wb(1)
+        for c in range(CHUNKS):
+            project(c)
+            if c + 2 < CHUNKS:
+                turn_wb(c + 2)
+            if c + 1 < CHUNKS:
+                quantise_wb(c + 1)
+            store(c)
+            if c + 2 < CHUNKS:
+                scale_wb(c + 2)

@@ -267,7 +267,10 @@ def tile_deepseekv3attention_pb_kernel(
             h0 = HEADS_PER_CHUNK * hg
             for m in range(TOKEN_TILES):
                 out_sb = outs.tile([P, CHUNK], F32, tag="out_sb")
-                nc.scalar.copy(out=out_sb[:], in_=kv_banks[m][:])
+                if m == TOKEN_TILES - 1:
+                    nc.vector.tensor_copy(out=out_sb[:], in_=kv_banks[m][:])
+                else:
+                    nc.scalar.copy(out=out_sb[:], in_=kv_banks[m][:])
                 nc.sync.dma_start(
                     out=(out_0, out_1)[kind][
                         P * m : P * m + P, h0 : h0 + HEADS_PER_CHUNK, :

@@ -12,6 +12,7 @@ ACT = mybir.ActivationFunctionType
 ALU = mybir.AluOpType
 
 P = 128
+HALF = P // 2
 TOKENS = 512
 HIDDEN = 2048
 LATENT = 512
@@ -20,14 +21,18 @@ HEAD_DIM = 128
 KINDS = 2
 EPS = 1e-6
 
-K_PASS = 512
+PACK = 4
+K_PASS = P * PACK
 PASSES_A = HIDDEN // K_PASS
 TOKEN_TILES = TOKENS // P
 LATENT_TILES = LATENT // P
-HEADS_PER_CHUNK = 4
+BANK = 512
+PSUM_BANKS = 8
+HEADS_PER_CHUNK = BANK // HEAD_DIM
 CHUNKS_PER_KIND = HEADS // HEADS_PER_CHUNK
 CHUNKS = KINDS * CHUNKS_PER_KIND
-CHUNK = HEADS_PER_CHUNK * HEAD_DIM
+FACTORS_A = (LATENT // P) * (HIDDEN // P)
+FACTORS_B = (HEADS * KINDS) * (LATENT // P)
 
 FLOPS = 2 * TOKENS * LATENT * HIDDEN + 2 * TOKENS * HEADS * KINDS * HEAD_DIM * LATENT
 
@@ -38,22 +43,26 @@ def tile_deepseekv3attention_pb_kernel(
     nc = tc.nc
     with ExitStack() as stack:
         const = stack.enter_context(tc.tile_pool(name="const", bufs=1))
-        raw = stack.enter_context(tc.tile_pool(name="raw", bufs=1))
-        keep = stack.enter_context(tc.tile_pool(name="keep", bufs=1))
-        work = stack.enter_context(tc.tile_pool(name="work", bufs=3))
-        stats = stack.enter_context(tc.tile_pool(name="stats", bufs=4))
-        outs = stack.enter_context(tc.tile_pool(name="outs", bufs=12))
-        turn = stack.enter_context(tc.psum_pool(name="turn", bufs=4))
-        acc = stack.enter_context(tc.psum_pool(name="acc", bufs=4))
+        loaded = stack.enter_context(tc.tile_pool(name="loaded", bufs=1))
+        quantised = stack.enter_context(tc.tile_pool(name="quantised", bufs=1))
+        per_token_tile = stack.enter_context(tc.tile_pool(name="per_token_tile", bufs=TOKEN_TILES))
+        per_chunk = stack.enter_context(tc.tile_pool(name="per_chunk", bufs=2))
+        outs = stack.enter_context(tc.tile_pool(name="outs", bufs=3 * TOKEN_TILES))
+        turn = stack.enter_context(tc.psum_pool(name="turn", bufs=PSUM_BANKS // 2))
+        acc = stack.enter_context(tc.psum_pool(name="acc", bufs=PSUM_BANKS // 2))
         stack.enter_context(tc.manual_schedule())
 
-        small_a = const.tile([P, 64], BF16, name="small_a")
+        small_a = const.tile([P, FACTORS_A], BF16, name="small_a")
         nc.vector.memset(small_a[:], 0.0)
         nc.sync.dma_start(out=small_a[0:1, :], in_=skv_a_lat.rearrange("(o a) b -> o (a b)", o=1))
-        small_b = const.tile([P, 768], BF16, name="small_b")
+        small_b = const.tile([P, 2 * FACTORS_B + LATENT], BF16, name="small_b")
         nc.vector.memset(small_b[:], 0.0)
-        nc.scalar.dma_start(out=small_b[0:1, 0:128], in_=skv_b.rearrange("(o a) b -> o (a b)", o=1))
-        nc.scalar.dma_start(out=small_b[0:1, 256:768], in_=kv_ln_w.rearrange("(o c) -> o c", o=1))
+        nc.scalar.dma_start(
+            out=small_b[0:1, 0:FACTORS_B], in_=skv_b.rearrange("(o a) b -> o (a b)", o=1)
+        )
+        nc.scalar.dma_start(
+            out=small_b[0:1, 2 * FACTORS_B :], in_=kv_ln_w.rearrange("(o c) -> o c", o=1)
+        )
         ones = const.tile([P, P], BF16, name="ones")
         nc.vector.memset(ones[:], 1.0)
         eps = const.tile([P, 1], F32, name="eps")
@@ -65,58 +74,70 @@ def tile_deepseekv3attention_pb_kernel(
 
         wa_raw = []
         for r in range(LATENT_TILES):
-            t = raw.tile([P, HIDDEN], BF16, name="wa_raw%d" % r)
-            nc.sync.dma_start(out=t[:], in_=wkv_a_lat[P * r : P * r + P, :])
-            wa_raw.append(t)
+            rows = loaded.tile([P, HIDDEN], BF16, name="wa_raw%d" % r)
+            nc.sync.dma_start(out=rows[:], in_=wkv_a_lat[P * r : P * r + P, :])
+            wa_raw.append(rows)
         x_raw = []
         for m in range(TOKEN_TILES):
-            t = raw.tile([P, HIDDEN], BF16, name="x_raw%d" % m)
-            nc.sync.dma_start(out=t[:], in_=hidden_states[P * m : P * m + P, :])
-            x_raw.append(t)
-        wb_rows = wkv_b.rearrange("(h k p) c -> p k h c", k=KINDS, p=P)
-        chunks = [(kind, hg) for kind in range(KINDS) for hg in range(CHUNKS_PER_KIND)]
+            rows = loaded.tile([P, HIDDEN], BF16, name="x_raw%d" % m)
+            nc.sync.dma_start(out=rows[:], in_=hidden_states[P * m : P * m + P, :])
+            x_raw.append(rows)
+        chunks = [(kind, group) for kind in range(KINDS) for group in range(CHUNKS_PER_KIND)]
+        wb_blocks = wkv_b.rearrange("(h k p) c -> p k h c", k=KINDS, p=P)
         wb_raw = []
-        for c, (kind, hg) in enumerate(chunks):
-            t = raw.tile([P, HEADS_PER_CHUNK, LATENT], BF16, name="wb_raw%d" % c)
-            h0 = HEADS_PER_CHUNK * hg
-            nc.sync.dma_start(out=t[:], in_=wb_rows[:, kind, h0 : h0 + HEADS_PER_CHUNK, :])
-            wb_raw.append(t)
+        for c, (kind, group) in enumerate(chunks):
+            rows = loaded.tile([P, HEADS_PER_CHUNK, LATENT], BF16, name="wb_raw%d" % c)
+            head = HEADS_PER_CHUNK * group
+            nc.sync.dma_start(out=rows[:], in_=wb_blocks[:, kind, head : head + HEADS_PER_CHUNK, :])
+            wb_raw.append(rows)
 
         def pick_factors(picked, spread, count):
-            for half in range(2):
-                rows = slice(64 * half, 64 * half + 64)
+            for odd in range(2):
+                half = slice(HALF * odd, HALF * odd + HALF)
                 nc.vector.tensor_copy(
-                    out=picked[rows],
-                    in_=spread[rows]
-                    .rearrange("p (x h) -> p x h", h=2)[:, :, half : half + 1]
-                    .to_broadcast([64, count, 2]),
+                    out=picked[half],
+                    in_=spread[half]
+                    .rearrange("p (x b) -> p x b", b=2)[:, :, odd : odd + 1]
+                    .to_broadcast([HALF, count, 2]),
                 )
 
-        sa_k = const.tile([P, LATENT_TILES, PASSES_A, 4], BF16, name="sa_k")
-        sa_ps = acc.tile([P, 64], F32, tag="acc")
+        sa_k = const.tile([P, LATENT_TILES, PASSES_A, PACK], BF16, name="sa_k")
+        sa_ps = acc.tile([P, FACTORS_A], F32, tag="acc")
         nc.tensor.matmul(out=sa_ps[:], lhsT=ones[:], rhs=small_a[:], start=True, stop=True)
-        pick_factors(sa_k[:].rearrange("p r g (u e) -> p (r g u) e", e=2), sa_ps[:], 32)
+        pick_factors(
+            sa_k[:].rearrange("p r g (u e) -> p (r g u) e", e=2), sa_ps[:], FACTORS_A // 2
+        )
 
-        sb_k = const.tile([P, HEADS, KINDS, 4], BF16, name="sb_k")
+        sb_k = const.tile([P, HEADS, KINDS, PACK], BF16, name="sb_k")
         gain = const.tile([P, LATENT], F32, name="gain")
 
         def spread_small_b():
-            sb_ps = acc.tile([P, 256], F32, tag="acc")
-            nc.tensor.matmul(out=sb_ps[:], lhsT=ones[:], rhs=small_b[:, 0:256], start=True, stop=True)
-            pick_factors(sb_k[:].rearrange("p h k (u e) -> p (h k u) e", e=2), sb_ps[:, 0:128], 64)
+            sb_ps = acc.tile([P, 2 * FACTORS_B], F32, tag="acc")
+            nc.tensor.matmul(
+                out=sb_ps[:], lhsT=ones[:], rhs=small_b[:, 0 : 2 * FACTORS_B], start=True, stop=True
+            )
+            pick_factors(
+                sb_k[:].rearrange("p h k (u e) -> p (h k u) e", e=2),
+                sb_ps[:, 0:FACTORS_B],
+                FACTORS_B // 2,
+            )
             gain_ps = acc.tile([P, LATENT], F32, tag="acc")
-            nc.tensor.matmul(out=gain_ps[:], lhsT=ones[:], rhs=small_b[:, 256:768], start=True, stop=True)
+            nc.tensor.matmul(
+                out=gain_ps[:], lhsT=ones[:], rhs=small_b[:, 2 * FACTORS_B :], start=True, stop=True
+            )
             nc.scalar.copy(out=gain[:], in_=gain_ps[:])
 
-        wa_grouped = keep.tile([P, PASSES_A, LATENT, 4], BF16, name="wa_grouped", align_bytes=64)
-        wa_codes = keep.tile([P, PASSES_A, LATENT], U32, name="wa_codes", align_bytes=64)
-        wa_scales = keep.tile([P, PASSES_A, LATENT], U8, name="wa_scales", align_bytes=64)
-        x_codes = keep.tile([P, TOKEN_TILES, PASSES_A, P], U32, name="x_codes", align_bytes=64)
-        x_scales = keep.tile([P, TOKEN_TILES, PASSES_A, P], U8, name="x_scales", align_bytes=64)
-        h_codes = keep.tile([P, TOKEN_TILES, P], U32, name="h_codes", align_bytes=64)
-        h_scales = keep.tile([P, TOKEN_TILES, P], U8, name="h_scales", align_bytes=64)
-        wb_codes = keep.tile([P, CHUNKS, CHUNK], U32, name="wb_codes", align_bytes=64)
-        wb_scales = keep.tile([P, CHUNKS, CHUNK], U8, name="wb_scales", align_bytes=64)
+        wa_grouped = quantised.tile(
+            [P, PASSES_A, LATENT, PACK], BF16, name="wa_grouped", align_bytes=64
+        )
+        wa_codes = quantised.tile([P, PASSES_A, LATENT], U32, name="wa_codes", align_bytes=64)
+        wa_scales = quantised.tile([P, PASSES_A, LATENT], U8, name="wa_scales", align_bytes=64)
+        x_codes = quantised.tile([P, TOKEN_TILES, PASSES_A, P], U32, name="x_codes", align_bytes=64)
+        x_scales = quantised.tile([P, TOKEN_TILES, PASSES_A, P], U8, name="x_scales", align_bytes=64)
+        h_codes = quantised.tile([P, TOKEN_TILES, P], U32, name="h_codes", align_bytes=64)
+        h_scales = quantised.tile([P, TOKEN_TILES, P], U8, name="h_scales", align_bytes=64)
+        wb_codes = quantised.tile([P, CHUNKS, BANK], U32, name="wb_codes", align_bytes=64)
+        wb_scales = quantised.tile([P, CHUNKS, BANK], U8, name="wb_scales", align_bytes=64)
 
         def turn_four(words, first):
             bank = turn.tile([P, 2, 2, P], F32, tag="turned")
@@ -139,10 +160,10 @@ def tile_deepseekv3attention_pb_kernel(
 
         def prepare_wa(r):
             words = wa_raw[r][:].bitcast(F32).rearrange("p (g w) -> p g w", g=PASSES_A)
-            for g0 in range(0, PASSES_A, 2):
-                bank = turn_four(words, g0)
+            for g in range(0, PASSES_A, 2):
+                bank = turn_four(words, g)
                 scale_out(
-                    bank, sa_k[:, r, g0 : g0 + 2, :], wa_grouped[:, g0 : g0 + 2, P * r : P * r + P, :]
+                    bank, sa_k[:, r, g : g + 2, :], wa_grouped[:, g : g + 2, P * r : P * r + P, :]
                 )
 
         def quantise_wa(g):
@@ -156,11 +177,13 @@ def tile_deepseekv3attention_pb_kernel(
 
         def turn_x(m):
             words = x_raw[m][:].bitcast(F32).rearrange("p (g w) -> p g w", g=PASSES_A)
-            grouped = stats.tile([P, PASSES_A, P, 4], BF16, tag="x_grouped", align_bytes=64)
-            for g0 in range(0, PASSES_A, 2):
-                bank = turn_four(words, g0)
+            grouped = per_token_tile.tile(
+                [P, PASSES_A, P, PACK], BF16, tag="x_grouped", align_bytes=64
+            )
+            for g in range(0, PASSES_A, 2):
+                bank = turn_four(words, g)
                 nc.scalar.copy(
-                    out=grouped[:].bitcast(F32)[:, g0 : g0 + 2, :, :],
+                    out=grouped[:].bitcast(F32)[:, g : g + 2, :, :],
                     in_=bank[:].rearrange("p u g j -> p g j u"),
                 )
             x_grouped[m] = grouped
@@ -186,16 +209,16 @@ def tile_deepseekv3attention_pb_kernel(
                     start=(g == 0),
                     stop=(g == PASSES_A - 1),
                 )
-            squares = stats.tile([P, LATENT], BF16, tag="squares")
-            sum_sq = stats.tile([P, 1], F32, tag="sum_sq")
+            squares = per_token_tile.tile([P, LATENT], BF16, tag="squares")
+            sum_sq = per_token_tile.tile([P, 1], F32, tag="sum_sq")
             nc.scalar.activation(out=squares[:], in_=lat[:], func=ACT.Square, accum_out=sum_sq[:])
-            rms = stats.tile([P, 1], F32, tag="rms")
+            rms = per_token_tile.tile([P, 1], F32, tag="rms")
             nc.scalar.activation(
                 out=rms[:], in_=sum_sq[:], func=ACT.Sqrt, scale=1.0 / LATENT, bias=eps[:]
             )
-            inv_rms = stats.tile([P, 1], F32, tag="inv_rms")
+            inv_rms = per_token_tile.tile([P, 1], F32, tag="inv_rms")
             nc.vector.reciprocal(out=inv_rms[:], in_=rms[:])
-            h_sb = stats.tile([P, LATENT], BF16, tag="h_sb")
+            h_sb = per_token_tile.tile([P, LATENT], BF16, tag="h_sb")
             nc.vector.scalar_tensor_tensor(
                 out=h_sb[:],
                 in0=lat[:],
@@ -213,7 +236,7 @@ def tile_deepseekv3attention_pb_kernel(
             bank = acc.tile([P, 2, P], F32, tag="acc")
             for u in range(2):
                 nc.tensor.transpose(bank[:, u, :], words[:, P * u : P * u + P], ident[:])
-            grouped = stats.tile([P, P, 4], BF16, tag="h_grouped", align_bytes=64)
+            grouped = per_token_tile.tile([P, P, PACK], BF16, tag="h_grouped", align_bytes=64)
             nc.scalar.copy(out=grouped[:].bitcast(F32), in_=bank[:].rearrange("p u j -> p j u"))
             h_grouped[m] = grouped
 
@@ -229,14 +252,18 @@ def tile_deepseekv3attention_pb_kernel(
 
         def turn_wb(c):
             words = wb_raw[c][:].bitcast(F32)
-            wb_banks[c] = [turn_four(words, i0) for i0 in range(0, HEADS_PER_CHUNK, 2)]
+            wb_banks[c] = [turn_four(words, i) for i in range(0, HEADS_PER_CHUNK, 2)]
 
         def scale_wb(c):
-            kind, hg = chunks[c]
-            grouped = work.tile([P, HEADS_PER_CHUNK, P, 4], BF16, tag="wb_grouped", align_bytes=64)
+            kind, group = chunks[c]
+            grouped = per_chunk.tile(
+                [P, HEADS_PER_CHUNK, P, PACK], BF16, tag="wb_grouped", align_bytes=64
+            )
             for b, bank in enumerate(wb_banks[c]):
-                h0 = HEADS_PER_CHUNK * hg + 2 * b
-                scale_out(bank, sb_k[:, h0 : h0 + 2, kind, :], grouped[:, 2 * b : 2 * b + 2, :, :])
+                head = HEADS_PER_CHUNK * group + 2 * b
+                scale_out(
+                    bank, sb_k[:, head : head + 2, kind, :], grouped[:, 2 * b : 2 * b + 2, :, :]
+                )
             wb_grouped[c] = grouped
 
         def quantise_wb(c):
@@ -250,7 +277,7 @@ def tile_deepseekv3attention_pb_kernel(
 
         def project(c):
             for m in range(TOKEN_TILES):
-                kv = acc.tile([P, CHUNK], F32, tag="acc")
+                kv = acc.tile([P, BANK], F32, tag="acc")
                 nc.tensor.matmul_mx(
                     out=kv[:],
                     lhsT=h_codes[:, m, :].bitcast(FP8X4),
@@ -263,34 +290,29 @@ def tile_deepseekv3attention_pb_kernel(
                 kv_banks[m] = kv
 
         def store(c):
-            kind, hg = chunks[c]
-            h0 = HEADS_PER_CHUNK * hg
+            kind, group = chunks[c]
+            head = HEADS_PER_CHUNK * group
             for m in range(TOKEN_TILES):
-                out_sb = outs.tile([P, CHUNK], F32, tag="out_sb")
-                if m == TOKEN_TILES - 1:
-                    nc.vector.tensor_copy(out=out_sb[:], in_=kv_banks[m][:])
-                else:
-                    nc.scalar.copy(out=out_sb[:], in_=kv_banks[m][:])
+                out_sb = outs.tile([P, BANK], F32, tag="out_sb")
+                nc.scalar.copy(out=out_sb[:], in_=kv_banks[m][:])
                 nc.sync.dma_start(
                     out=(out_0, out_1)[kind][
-                        P * m : P * m + P, h0 : h0 + HEADS_PER_CHUNK, :
+                        P * m : P * m + P, head : head + HEADS_PER_CHUNK, :
                     ].rearrange("p h d -> p (h d)"),
                     in_=out_sb[:],
                 )
 
         for r in range(LATENT_TILES):
             prepare_wa(r)
-        spread_small_b()
         turn_x(0)
         turn_x(1)
         for g in range(PASSES_A):
             quantise_wa(g)
-        quantise_x(0)
-        turn_x(2)
-        quantise_x(1)
-        turn_x(3)
-        quantise_x(2)
-        quantise_x(3)
+        for m in range(TOKEN_TILES):
+            quantise_x(m)
+            if m + 2 < TOKEN_TILES:
+                turn_x(m + 2)
+        spread_small_b()
         for m in range(TOKEN_TILES):
             latent(m)
         turn_wb(0)

from contextlib import ExitStack

import concourse.mybir as mybir
from concourse.masks import make_identity

F32 = mybir.dt.float32
BF16 = mybir.dt.bfloat16
U32 = mybir.dt.uint32
U8 = mybir.dt.uint8
FP8X4 = mybir.dt.float8_e4m3fn_x4
ACT = mybir.ActivationFunctionType
ALU = mybir.AluOpType

P = 128
HALF = P // 2
TOKENS = 512
HIDDEN = 2048
LATENT = 512
HEADS = 16
HEAD_DIM = 128
KINDS = 2
EPS = 1e-6

PACK = 4
K_PASS = P * PACK
PASSES_A = HIDDEN // K_PASS
TOKEN_TILES = TOKENS // P
LATENT_TILES = LATENT // P
BANK = 512
PSUM_BANKS = 8
HEADS_PER_CHUNK = BANK // HEAD_DIM
CHUNKS_PER_KIND = HEADS // HEADS_PER_CHUNK
CHUNKS = KINDS * CHUNKS_PER_KIND
FACTORS_A = (LATENT // P) * (HIDDEN // P)
FACTORS_B = (HEADS * KINDS) * (LATENT // P)

FLOPS = 2 * TOKENS * LATENT * HIDDEN + 2 * TOKENS * HEADS * KINDS * HEAD_DIM * LATENT


def tile_deepseekv3attention_pb_kernel(
    tc, hidden_states, wkv_a_lat, skv_a_lat, wkv_b, skv_b, kv_ln_w, out_0, out_1
):
    nc = tc.nc
    with ExitStack() as stack:
        const = stack.enter_context(tc.tile_pool(name="const", bufs=1))
        loaded = stack.enter_context(tc.tile_pool(name="loaded", bufs=1))
        quantised = stack.enter_context(tc.tile_pool(name="quantised", bufs=1))
        per_token_tile = stack.enter_context(tc.tile_pool(name="per_token_tile", bufs=TOKEN_TILES))
        per_chunk = stack.enter_context(tc.tile_pool(name="per_chunk", bufs=2))
        outs = stack.enter_context(tc.tile_pool(name="outs", bufs=3 * TOKEN_TILES))
        turn = stack.enter_context(tc.psum_pool(name="turn", bufs=PSUM_BANKS // 2))
        acc = stack.enter_context(tc.psum_pool(name="acc", bufs=PSUM_BANKS // 2))
        stack.enter_context(tc.manual_schedule())

        small_a = const.tile([P, FACTORS_A], BF16, name="small_a")
        nc.vector.memset(small_a[:], 0.0)
        nc.sync.dma_start(out=small_a[0:1, :], in_=skv_a_lat.rearrange("(o a) b -> o (a b)", o=1))
        small_b = const.tile([P, 2 * FACTORS_B + LATENT], BF16, name="small_b")
        nc.vector.memset(small_b[:], 0.0)
        nc.scalar.dma_start(
            out=small_b[0:1, 0:FACTORS_B], in_=skv_b.rearrange("(o a) b -> o (a b)", o=1)
        )
        nc.scalar.dma_start(
            out=small_b[0:1, 2 * FACTORS_B :], in_=kv_ln_w.rearrange("(o c) -> o c", o=1)
        )
        ones = const.tile([P, P], BF16, name="ones")
        nc.vector.memset(ones[:], 1.0)
        eps = const.tile([P, 1], F32, name="eps")
        nc.vector.memset(eps[:], EPS)
        warm = const.tile([P, 1], F32, name="warm")
        nc.scalar.activation(out=warm[:], in_=eps[:], func=ACT.Sqrt)
        ident = const.tile([P, P], F32, name="ident")
        make_identity(nc, ident[:])

        wa_raw = []
        for r in range(LATENT_TILES):
            rows = loaded.tile([P, HIDDEN], BF16, name="wa_raw%d" % r)
            nc.sync.dma_start(out=rows[:], in_=wkv_a_lat[P * r : P * r + P, :])
            wa_raw.append(rows)
        x_raw = []
        for m in range(TOKEN_TILES):
            rows = loaded.tile([P, HIDDEN], BF16, name="x_raw%d" % m)
            nc.sync.dma_start(out=rows[:], in_=hidden_states[P * m : P * m + P, :])
            x_raw.append(rows)
        chunks = [(kind, group) for kind in range(KINDS) for group in range(CHUNKS_PER_KIND)]
        wb_blocks = wkv_b.rearrange("(h k p) c -> p k h c", k=KINDS, p=P)
        wb_raw = []
        for c, (kind, group) in enumerate(chunks):
            rows = loaded.tile([P, HEADS_PER_CHUNK, LATENT], BF16, name="wb_raw%d" % c)
            head = HEADS_PER_CHUNK * group
            nc.sync.dma_start(out=rows[:], in_=wb_blocks[:, kind, head : head + HEADS_PER_CHUNK, :])
            wb_raw.append(rows)

        def pick_factors(picked, spread, count):
            for odd in range(2):
                half = slice(HALF * odd, HALF * odd + HALF)
                nc.vector.tensor_copy(
                    out=picked[half],
                    in_=spread[half]
                    .rearrange("p (x b) -> p x b", b=2)[:, :, odd : odd + 1]
                    .to_broadcast([HALF, count, 2]),
                )

        sa_k = const.tile([P, LATENT_TILES, PASSES_A, PACK], BF16, name="sa_k")
        sa_ps = acc.tile([P, FACTORS_A], F32, tag="acc")
        nc.tensor.matmul(out=sa_ps[:], lhsT=ones[:], rhs=small_a[:], start=True, stop=True)
        pick_factors(
            sa_k[:].rearrange("p r g (u e) -> p (r g u) e", e=2), sa_ps[:], FACTORS_A // 2
        )

        sb_k = const.tile([P, HEADS, KINDS, PACK], BF16, name="sb_k")
        gain = const.tile([P, LATENT], F32, name="gain")

        def spread_small_b():
            sb_ps = acc.tile([P, 2 * FACTORS_B], F32, tag="acc")
            nc.tensor.matmul(
                out=sb_ps[:], lhsT=ones[:], rhs=small_b[:, 0 : 2 * FACTORS_B], start=True, stop=True
            )
            pick_factors(
                sb_k[:].rearrange("p h k (u e) -> p (h k u) e", e=2),
                sb_ps[:, 0:FACTORS_B],
                FACTORS_B // 2,
            )
            gain_ps = acc.tile([P, LATENT], F32, tag="acc")
            nc.tensor.matmul(
                out=gain_ps[:], lhsT=ones[:], rhs=small_b[:, 2 * FACTORS_B :], start=True, stop=True
            )
            nc.scalar.copy(out=gain[:], in_=gain_ps[:])

        wa_grouped = quantised.tile(
            [P, PASSES_A, LATENT, PACK], BF16, name="wa_grouped", align_bytes=64
        )
        wa_codes = quantised.tile([P, PASSES_A, LATENT], U32, name="wa_codes", align_bytes=64)
        wa_scales = quantised.tile([P, PASSES_A, LATENT], U8, name="wa_scales", align_bytes=64)
        x_codes = quantised.tile([P, TOKEN_TILES, PASSES_A, P], U32, name="x_codes", align_bytes=64)
        x_scales = quantised.tile([P, TOKEN_TILES, PASSES_A, P], U8, name="x_scales", align_bytes=64)
        h_codes = quantised.tile([P, TOKEN_TILES, P], U32, name="h_codes", align_bytes=64)
        h_scales = quantised.tile([P, TOKEN_TILES, P], U8, name="h_scales", align_bytes=64)
        wb_codes = quantised.tile([P, CHUNKS, BANK], U32, name="wb_codes", align_bytes=64)
        wb_scales = quantised.tile([P, CHUNKS, BANK], U8, name="wb_scales", align_bytes=64)

        def turn_four(words, first):
            bank = turn.tile([P, 2, 2, P], F32, tag="turned")
            for i in range(2):
                for u in range(2):
                    nc.tensor.transpose(
                        bank[:, u, i, :], words[:, first + i, P * u : P * u + P], ident[:]
                    )
            return bank

        def scale_out(bank, factors, grouped):
            nc.vector.tensor_tensor(
                out=grouped.rearrange("p i j (u e) -> p i j u e", e=2),
                in0=bank[:].bitcast(BF16).rearrange("p u i (j e) -> p i j u e", e=2),
                in1=factors.rearrange("p i (u e) -> p i u e", e=2)
                .unsqueeze(2)
                .to_broadcast([P, 2, P, 2, 2]),
                op=ALU.mult,
            )

        def prepare_wa(r):
            words = wa_raw[r][:].bitcast(F32).rearrange("p (g w) -> p g w", g=PASSES_A)
            for g in range(0, PASSES_A, 2):
                bank = turn_four(words, g)
                scale_out(
                    bank, sa_k[:, r, g : g + 2, :], wa_grouped[:, g : g + 2, P * r : P * r + P, :]
                )

        def quantise_wa(g):
            nc.vector.quantize_mx(
                out=wa_codes[:, g, :].bitcast(FP8X4),
                scales=wa_scales[:, g, :],
                in_=wa_grouped[:, g, :, :].rearrange("p o t -> p (o t)"),
            )

        x_grouped = {}

        def turn_x(m):
            words = x_raw[m][:].bitcast(F32).rearrange("p (g w) -> p g w", g=PASSES_A)
            grouped = per_token_tile.tile(
                [P, PASSES_A, P, PACK], BF16, tag="x_grouped", align_bytes=64
            )
            for g in range(0, PASSES_A, 2):
                bank = turn_four(words, g)
                nc.scalar.copy(
                    out=grouped[:].bitcast(F32)[:, g : g + 2, :, :],
                    in_=bank[:].rearrange("p u g j -> p g j u"),
                )
            x_grouped[m] = grouped

        def quantise_x(m):
            nc.vector.quantize_mx(
                out=x_codes[:, m, :, :].rearrange("p g j -> p (g j)").bitcast(FP8X4),
                scales=x_scales[:, m, :, :].rearrange("p g j -> p (g j)"),
                in_=x_grouped[m][:].rearrange("p g j t -> p (g j t)"),
            )

        h_rows = {}

        def latent(m):
            lat = acc.tile([P, LATENT], F32, tag="acc")
            for g in range(PASSES_A):
                nc.tensor.matmul_mx(
                    out=lat[:],
                    lhsT=x_codes[:, m, g, :].bitcast(FP8X4),
                    lhsT_scale=x_scales[:, m, g, :],
                    rhs=wa_codes[:, g, :].bitcast(FP8X4),
                    rhs_scale=wa_scales[:, g, :],
                    start=(g == 0),
                    stop=(g == PASSES_A - 1),
                )
            squares = per_token_tile.tile([P, LATENT], BF16, tag="squares")
            sum_sq = per_token_tile.tile([P, 1], F32, tag="sum_sq")
            nc.scalar.activation(out=squares[:], in_=lat[:], func=ACT.Square, accum_out=sum_sq[:])
            rms = per_token_tile.tile([P, 1], F32, tag="rms")
            nc.scalar.activation(
                out=rms[:], in_=sum_sq[:], func=ACT.Sqrt, scale=1.0 / LATENT, bias=eps[:]
            )
            inv_rms = per_token_tile.tile([P, 1], F32, tag="inv_rms")
            nc.vector.reciprocal(out=inv_rms[:], in_=rms[:])
            h_sb = per_token_tile.tile([P, LATENT], BF16, tag="h_sb")
            nc.vector.scalar_tensor_tensor(
                out=h_sb[:],
                in0=lat[:],
                scalar=inv_rms[:],
                in1=gain[:],
                op0=ALU.mult,
                op1=ALU.mult,
            )
            h_rows[m] = h_sb

        h_grouped = {}

        def turn_h(m):
            words = h_rows[m][:].bitcast(F32)
            bank = acc.tile([P, 2, P], F32, tag="acc")
            for u in range(2):
                nc.tensor.transpose(bank[:, u, :], words[:, P * u : P * u + P], ident[:])
            grouped = per_token_tile.tile([P, P, PACK], BF16, tag="h_grouped", align_bytes=64)
            nc.scalar.copy(out=grouped[:].bitcast(F32), in_=bank[:].rearrange("p u j -> p j u"))
            h_grouped[m] = grouped

        def quantise_h(m):
            nc.vector.quantize_mx(
                out=h_codes[:, m, :].bitcast(FP8X4),
                scales=h_scales[:, m, :],
                in_=h_grouped[m][:].rearrange("p j t -> p (j t)"),
            )

        wb_banks = {}
        wb_grouped = {}

        def turn_wb(c):
            words = wb_raw[c][:].bitcast(F32)
            wb_banks[c] = [turn_four(words, i) for i in range(0, HEADS_PER_CHUNK, 2)]

        def scale_wb(c):
            kind, group = chunks[c]
            grouped = per_chunk.tile(
                [P, HEADS_PER_CHUNK, P, PACK], BF16, tag="wb_grouped", align_bytes=64
            )
            for b, bank in enumerate(wb_banks[c]):
                head = HEADS_PER_CHUNK * group + 2 * b
                scale_out(
                    bank, sb_k[:, head : head + 2, kind, :], grouped[:, 2 * b : 2 * b + 2, :, :]
                )
            wb_grouped[c] = grouped

        def quantise_wb(c):
            nc.vector.quantize_mx(
                out=wb_codes[:, c, :].bitcast(FP8X4),
                scales=wb_scales[:, c, :],
                in_=wb_grouped[c][:].rearrange("p i j t -> p (i j t)"),
            )

        kv_banks = {}

        def project(c):
            for m in range(TOKEN_TILES):
                kv = acc.tile([P, BANK], F32, tag="acc")
                nc.tensor.matmul_mx(
                    out=kv[:],
                    lhsT=h_codes[:, m, :].bitcast(FP8X4),
                    lhsT_scale=h_scales[:, m, :],
                    rhs=wb_codes[:, c, :].bitcast(FP8X4),
                    rhs_scale=wb_scales[:, c, :],
                    start=True,
                    stop=True,
                )
                kv_banks[m] = kv

        def store(c):
            kind, group = chunks[c]
            head = HEADS_PER_CHUNK * group
            for m in range(TOKEN_TILES):
                out_sb = outs.tile([P, BANK], F32, tag="out_sb")
                nc.scalar.copy(out=out_sb[:], in_=kv_banks[m][:])
                nc.sync.dma_start(
                    out=(out_0, out_1)[kind][
                        P * m : P * m + P, head : head + HEADS_PER_CHUNK, :
                    ].rearrange("p h d -> p (h d)"),
                    in_=out_sb[:],
                )

        for r in range(LATENT_TILES):
            prepare_wa(r)
        turn_x(0)
        turn_x(1)
        for g in range(PASSES_A):
            quantise_wa(g)
        for m in range(TOKEN_TILES):
            quantise_x(m)
            if m + 2 < TOKEN_TILES:
                turn_x(m + 2)
        spread_small_b()
        for m in range(TOKEN_TILES):
            latent(m)
        turn_wb(0)
        turn_wb(1)
        for m in range(TOKEN_TILES):
            turn_h(m)
        scale_wb(0)
        quantise_h(0)
        quantise_h(1)
        quantise_wb(0)
        quantise_h(2)
        quantise_h(3)
        scale_wb(1)
        for c in range(CHUNKS):
            project(c)
            if c + 2 < CHUNKS:
                turn_wb(c + 2)
            if c + 1 < CHUNKS:
                quantise_wb(c + 1)
            store(c)
            if c + 2 < CHUNKS:
                scale_wb(c + 2)
